import numpy as np
import ml_dtypes


def mxq(x, axis, fmt="e4m3"):
    dtype, down = {"e4m3": (ml_dtypes.float8_e4m3fn, 7), "e5m2": (ml_dtypes.float8_e5m2, 14)}[fmt]
    v = np.moveaxis(np.asarray(x, np.float32).astype(ml_dtypes.bfloat16).astype(np.float64), axis, -1)
    blocks = v.reshape(v.shape[:-1] + (-1, 32))
    amax = np.abs(blocks).max(-1, keepdims=True)
    byte = np.maximum(np.where(amax > 0, np.frexp(amax)[1] - 1 + 127, 0) - down, 1)
    scale = np.exp2(byte - 127.0)
    codes = (blocks / scale).astype(np.float32).astype(dtype).astype(np.float64)
    return np.moveaxis((codes * scale).reshape(v.shape), -1, axis)


WIDE = False


def mx_kscale(k):
    if not WIDE:
        return np.ones(k)
    levels = np.array([18, -18])
    if k % 512:
        return np.exp2(np.random.permutation(np.resize(levels, k // 32))).repeat(32)
    a = np.empty((k // 512, 16))
    for p in range(k // 512):
        a[p, :8] = np.random.permutation(np.resize(levels, 8))
        for g in range(8):
            far = levels[np.abs(levels - a[p, g]) >= 10]
            a[p, g + 8] = far[np.random.randint(len(far))]
    return np.exp2(a.ravel()).repeat(32)


BF16 = ml_dtypes.bfloat16


def bf(x):
    return np.asarray(x, np.float32).astype(BF16)


def f64(x):
    return np.asarray(x).astype(np.float64)


B, N, D = 3, 512, 512


def setup_inputs():
    a = mx_kscale(N)
    v = mx_kscale(D)
    c = mx_kscale(B * N).reshape(B, N)
    xwx0 = bf(np.abs(np.random.standard_normal((B, N, N))) * 2.0)
    inp0 = bf(np.random.standard_normal((B, N, D)) / np.sqrt(N))
    V0 = bf(np.random.standard_normal((D, D)) * 1.5 * np.sqrt(N / D))
    x = bf(np.random.standard_normal((B, N, D)))
    g = bf(np.random.standard_normal((B, N, D)) * np.exp2(np.random.randint(-6, 1, (B, N, 1))) * 4.0 / a[None, :, None] * v)
    u = f64(inp0) @ f64(V0).T
    sc = f64(xwx0)
    mx = sc.max(-1, keepdims=True)
    lse = (mx + np.log(np.exp(sc - mx).sum(-1, keepdims=True)))[:, :, 0]
    return {"xwx": bf(sc + np.log(a)[None, :, None] - np.log(c)[:, None, :]),
            "inp": bf(f64(inp0) * c[:, :, None]),
            "V": bf(f64(V0) / v[:, None]),
            "x": x,
            "u": np.asarray(u, np.float32),
            "lse": np.asarray(lse, np.float32),
            "grad_out": g}


def reference(xwx, inp, V, x, u, lse, grad_out):
    uf = f64(u)
    p = np.exp(f64(xwx) - f64(lse)[:, :, None])
    dh = mxq(p, 1, "e4m3").transpose(0, 2, 1) @ mxq(f64(grad_out), 1, "e5m2")
    dz1 = (dh * (uf / np.sqrt(np.square(uf) + 1e-8))).reshape(B * N, D)
    dinp = mxq(dz1, 1, "e5m2") @ mxq(f64(V), 0, "e4m3")
    dV = mxq(dz1, 0, "e5m2").T @ mxq(f64(inp).reshape(B * N, D), 0, "e4m3")
    return dinp.reshape(B, N, D), dV

@@ -1,0 +1,312 @@
+from contextlib import ExitStack
+
+import concourse.mybir as mybir
+from concourse.masks import make_identity
+
+B, N, D = 3, 512, 512
+FLOPS = 3 * B * 2 * N * N * D
+BYTES = 3 * B * N * D * 2 + D * D * 2 + B * N * D * 4 + B * N * 4 + B * N * D * 4 + D * D * 4
+
+F32 = mybir.dt.float32
+BF16 = mybir.dt.bfloat16
+U32 = mybir.dt.uint32
+U8 = mybir.dt.uint8
+E4M3 = mybir.dt.float8_e4m3fn_x4
+E5M2 = mybir.dt.float8_e5m2_x4
+ACT = mybir.ActivationFunctionType
+ALU = mybir.AluOpType
+
+P = 128
+PACK = 4
+W = 512
+WIDE = PACK * W
+EPS = 1e-8
+
+
+def tile_quantumattentionblock_pb_v_kernel(tc, xwx, inp, V, x, u, lse, grad_out, out_0, out_1):
+    nc = tc.nc
+    with ExitStack() as ctx:
+        keep = ctx.enter_context(tc.tile_pool(name="keep", bufs=1))
+        stage = ctx.enter_context(tc.tile_pool(name="stage", bufs=4))
+        psum = ctx.enter_context(tc.psum_pool(name="psum", bufs=1))
+        ctx.enter_context(tc.manual_schedule())
+
+        def kept(name, width, dtype):
+            return keep.tile([P, width], dtype, name=name, align_bytes=64)
+
+        def rows4(ap):
+            return ap.rearrange("(p j) w -> p (j w)", j=PACK)
+
+        x_sb = [kept("x%d" % b, WIDE, BF16) for b in range(B)]
+        g_sb = [kept("g%d" % b, WIDE, BF16) for b in range(B)]
+        i_sb = [kept("i%d" % b, WIDE, BF16) for b in range(B)]
+        u_sb = [kept("u%d" % b, WIDE, F32) for b in range(B)]
+        s_sb = [kept("s%d" % b, WIDE, F32) for b in range(B)]
+        p_sb = [kept("p%d" % b, WIDE, BF16) for b in range(B)]
+        z_sb = [kept("z%d" % b, WIDE, BF16) for b in range(B)]
+        f_sb = [kept("f%d" % b, WIDE, BF16) for b in range(B)]
+        o_sb = [kept("o%d" % b, WIDE, F32) for b in range(B)]
+        dv_sb = kept("dv", WIDE, F32)
+        v_sb = kept("v", WIDE, BF16)
+        lse_sb = kept("lse", B * 8, F32)
+        neg_lse = kept("neg_lse", B * 8, F32)
+        ident = kept("ident", P, F32)
+        warm = kept("warm", 16, F32)
+        codes = {}
+        scales = {}
+        for key in ["v"] + [kind + str(b) for kind in "pgitf" for b in range(B)]:
+            codes[key] = kept("codes_" + key, W, U32)
+            scales[key] = kept("scales_" + key, W, U8)
+        grouped = {}
+        banks = {}
+
+        half = WIDE // 2
+
+        def load(dst, src, parts=1):
+            step = WIDE // parts
+            for c in range(0, WIDE, step):
+                nc.sync.dma_start(out=dst[:, c : c + step], in_=rows4(src)[:, c : c + step])
+
+        lse_view = lse_sb[:].rearrange("p (b e) -> p b e", e=8)[:, :, 0:PACK]
+        neg_view = neg_lse[:].rearrange("p (b e) -> p b e", e=8)[:, :, 0:PACK]
+        nc.scalar.dma_start(out=lse_view, in_=lse.rearrange("b (p j) -> p b j", j=PACK))
+        load(g_sb[0], grad_out[0])
+        load(x_sb[0], xwx[0], 2)
+        load(g_sb[1], grad_out[1])
+        load(x_sb[1], xwx[1])
+        load(x_sb[2], xwx[2])
+        load(g_sb[2], grad_out[2])
+        load(u_sb[0], u[0], 2)
+        load(v_sb, V)
+        load(i_sb[0], inp[0])
+        load(u_sb[1], u[1])
+        load(i_sb[1], inp[1])
+        load(u_sb[2], u[2])
+        load(i_sb[2], inp[2])
+
+        nc.vector.memset(warm[:, 0:8], 0.0)
+        nc.scalar.activation(out=warm[:, 8:16], in_=warm[:, 0:8], func=ACT.Exp)
+        make_identity(nc, ident[:])
+        nc.vector.tensor_scalar(out=neg_view, in0=lse_view, scalar1=-1.0, scalar2=None, op0=ALU.mult)
+
+        def probabilities(b):
+            for j in range(PACK):
+                cols = slice(j * W, (j + 1) * W)
+                nc.scalar.activation(
+                    out=p_sb[b][:, cols].rearrange("p (t m) -> p t m", t=PACK),
+                    in_=x_sb[b][:, cols].rearrange("p (m t) -> p t m", t=PACK),
+                    func=ACT.Exp,
+                    bias=neg_lse[:, 8 * b + j : 8 * b + j + 1],
+                )
+
+        def interleave(key, src, on_scalar=False):
+            dst = stage.tile([P, WIDE], BF16, name="grouped", align_bytes=64)
+            grouped[key] = dst
+            out = dst[:].rearrange("p (c i j) -> p c j i", i=4, j=PACK)
+            in_ = src[:].rearrange("p (j c i) -> p c j i", i=4, j=PACK)
+            if on_scalar:
+                nc.scalar.copy(out=out, in_=in_)
+            else:
+                nc.vector.tensor_copy(out=out, in_=in_)
+
+        def quantize(key, fmt, part=0, parts=1):
+            step = W // parts
+            cols = slice(part * step, (part + 1) * step)
+            nc.vector.quantize_mx(
+                out=codes[key][:, cols].bitcast(fmt),
+                scales=scales[key][:, cols],
+                in_=grouped[key][:, PACK * part * step : PACK * (part + 1) * step],
+            )
+
+        def bank(tag):
+            return psum.tile([P, W], F32, name=tag)
+
+        def product(acc, left, left_fmt, chunk, right, right_fmt, start=True, stop=True):
+            cols = slice(chunk * P, (chunk + 1) * P)
+            nc.tensor.matmul_mx(
+                out=acc[:],
+                lhsT=codes[left][:, cols].bitcast(left_fmt),
+                lhsT_scale=scales[left][:, cols],
+                rhs=codes[right][:].bitcast(right_fmt),
+                rhs_scale=scales[right][:],
+                start=start,
+                stop=stop,
+            )
+
+        def dh_products(b):
+            for t in range(PACK):
+                banks["dh", t] = bank("wide%d" % t)
+                product(banks["dh", t], "p%d" % b, E4M3, t, "g%d" % b, E5M2)
+
+        def square(b, h):
+            cols = slice(h * half, (h + 1) * half)
+            nc.scalar.activation(out=s_sb[b][:, cols], in_=u_sb[b][:, cols], func=ACT.Square)
+
+        def inverse_root(b, h):
+            cols = slice(h * half, (h + 1) * half)
+            nc.scalar.activation(out=s_sb[b][:, cols], in_=s_sb[b][:, cols], func=ACT.Abs_reciprocal_sqrt, bias=EPS)
+
+        def slope(b, h):
+            cols = slice(h * half, (h + 1) * half)
+            nc.vector.tensor_tensor(out=s_sb[b][:, cols], in0=u_sb[b][:, cols], in1=s_sb[b][:, cols], op=ALU.mult)
+
+        def dz(b, t):
+            cols = slice(t * W, (t + 1) * W)
+            nc.vector.tensor_tensor(
+                out=z_sb[b][:, cols].rearrange("p (h w e) -> p h w e", h=2, e=2),
+                in0=banks["dh", t][:].rearrange("p (w h e) -> p h w e", h=2, e=2),
+                in1=s_sb[b][:, cols].rearrange("p (w h e) -> p h w e", h=2, e=2),
+                op=ALU.mult,
+            )
+
+        def transposes(b, pair):
+            words = z_sb[b][:].bitcast(F32)
+            banks["tr", pair] = bank("turn%d" % pair)
+            for q in range(4):
+                c = (4 * pair + q) * P
+                nc.tensor.transpose(banks["tr", pair][:, q * P : (q + 1) * P], words[:, c : c + P], ident[:])
+
+        def feature_copy(b, pair):
+            grouped["f%d" % b] = f_sb[b]
+            nc.scalar.copy(
+                out=f_sb[b][:, pair * half : (pair + 1) * half].bitcast(F32).rearrange("p (t m h) -> p t m h", t=2, h=2),
+                in_=banks["tr", pair][:].rearrange("p (t h m) -> p t m h", t=2, h=2),
+            )
+
+        def token_interleave(b, h, on_scalar=False):
+            key = "t%d%d" % (b, h)
+            grouped[key] = stage.tile([P, half], BF16, name="grouped_half", align_bytes=64)
+            copy = nc.scalar.copy if on_scalar else nc.vector.tensor_copy
+            copy(
+                out=grouped[key][:].rearrange("p (e c a t) -> p c t a e", e=2, a=2, t=PACK),
+                in_=z_sb[b][:].rearrange("p (t h c a e) -> p h c t a e", t=PACK, h=2, a=2, e=2)[:, h],
+            )
+
+        def token_quantize(b, h):
+            cols = slice(h * W // 2, (h + 1) * W // 2)
+            nc.vector.quantize_mx(
+                out=codes["t%d" % b][:, cols].bitcast(E5M2),
+                scales=scales["t%d" % b][:, cols],
+                in_=grouped["t%d%d" % (b, h)][:],
+            )
+
+        def dinp(b, t, on_vector=False):
+            acc = bank(("out0", "out1", "turn0", "turn1")[t])
+            product(acc, "f%d" % b, E5M2, t, "v", E4M3)
+            cols = slice(t * W, (t + 1) * W)
+            if on_vector:
+                nc.vector.tensor_copy(out=o_sb[b][:, cols], in_=acc[:])
+            else:
+                nc.scalar.copy(out=o_sb[b][:, cols], in_=acc[:])
+
+        def store_dinp(b, first, count):
+            cols = slice(first * W, (first + count) * W)
+            nc.sync.dma_start(out=rows4(out_0[b])[:, cols], in_=o_sb[b][:, cols])
+
+        def dv_pass(c, b, last=False):
+            if b == 0:
+                banks["dv", c] = bank("wide%d" % c)
+            product(banks["dv", c], "t%d" % b, E5M2, c, "i%d" % b, E4M3, start=(b == 0), stop=last)
+
+        def dv_out(c, on_vector):
+            cols = slice(c * W, (c + 1) * W)
+            if on_vector:
+                nc.vector.tensor_copy(out=dv_sb[:, cols], in_=banks["dv", c][:])
+            else:
+                nc.scalar.copy(out=dv_sb[:, cols], in_=banks["dv", c][:])
+            nc.sync.dma_start(out=rows4(out_1)[:, cols], in_=dv_sb[:, cols])
+
+        interleave("g0", g_sb[0])
+        probabilities(0)
+        quantize("g0", E5M2)
+        interleave("g1", g_sb[1])
+        interleave("p0", p_sb[0])
+        quantize("g1", E5M2)
+        quantize("p0", E4M3)
+        dh_products(0)
+        probabilities(1)
+        interleave("p1", p_sb[1])
+        interleave("g2", g_sb[2])
+        quantize("p1", E4M3)
+        quantize("g2", E5M2)
+        probabilities(2)
+        square(0, 0)
+        square(0, 1)
+        inverse_root(0, 0)
+        inverse_root(0, 1)
+        interleave("p2", p_sb[2])
+        interleave("v", v_sb)
+        quantize("p2", E4M3)
+        slope(0, 0)
+        quantize("v", E4M3)
+        slope(0, 1)
+        square(1, 0)
+        square(1, 1)
+        inverse_root(1, 0)
+        inverse_root(1, 1)
+        for t in range(PACK):
+            dz(0, t)
+            if t % 2:
+                transposes(0, t // 2)
+        dh_products(1)
+        feature_copy(0, 0)
+        feature_copy(0, 1)
+        square(2, 0)
+        square(2, 1)
+        slope(1, 0)
+        slope(1, 1)
+        quantize("f0", E5M2)
+        for t in range(PACK):
+            dinp(0, t)
+        store_dinp(0, 0, PACK)
+        for t in range(PACK):
+            dz(1, t)
+            if t % 2:
+                transposes(1, t // 2)
+        dh_products(2)
+        inverse_root(2, 0)
+        feature_copy(1, 0)
+        feature_copy(1, 1)
+        inverse_root(2, 1)
+        interleave("i0", i_sb[0], on_scalar=True)
+        token_interleave(0, 0)
+        token_interleave(0, 1)
+        token_quantize(0, 0)
+        token_quantize(0, 1)
+        slope(2, 0)
+        quantize("f1", E5M2)
+        interleave("i1", i_sb[1])
+        slope(2, 1)
+        quantize("i1", E4M3)
+        for t in range(PACK):
+            dinp(1, t)
+        store_dinp(1, 0, PACK)
+        for t in range(PACK):
+            dz(2, t)
+            if t % 2:
+                transposes(2, t // 2)
+                feature_copy(2, t // 2)
+        token_interleave(2, 0, on_scalar=True)
+        token_interleave(2, 1, on_scalar=True)
+        quantize("i0", E4M3)
+        for c in range(PACK):
+            dv_pass(c, 0)
+        interleave("i2", i_sb[2])
+        quantize("f2", E5M2)
+        quantize("i2", E4M3)
+        for t in range(PACK):
+            dinp(2, t)
+            if t % 2:
+                store_dinp(2, t - 1, 2)
+        token_interleave(1, 0)
+        token_quantize(2, 0)
+        token_interleave(1, 1)
+        token_quantize(2, 1)
+        for c in range(PACK):
+            dv_pass(c, 2)
+        token_quantize(1, 0)
+        token_quantize(1, 1)
+        for c in range(PACK):
+            dv_pass(c, 1, last=True)
+        for c in range(PACK):
+            dv_out(c, on_vector=(c % 2 == 0))

@@ -27,7 +27,7 @@ def tile_quantumattentionblock_pb_v_kernel(tc, xwx, inp, V, x, u, lse, grad_out,
     nc = tc.nc
     with ExitStack() as ctx:
         keep = ctx.enter_context(tc.tile_pool(name="keep", bufs=1))
-        stage = ctx.enter_context(tc.tile_pool(name="stage", bufs=4))
+        stage = ctx.enter_context(tc.tile_pool(name="stage", bufs=5))
         psum = ctx.enter_context(tc.psum_pool(name="psum", bufs=1))
         ctx.enter_context(tc.manual_schedule())
 
@@ -42,14 +42,17 @@ def tile_quantumattentionblock_pb_v_kernel(tc, xwx, inp, V, x, u, lse, grad_out,
         i_sb = [kept("i%d" % b, WIDE, BF16) for b in range(B)]
         u_sb = [kept("u%d" % b, WIDE, F32) for b in range(B)]
         s_sb = [kept("s%d" % b, WIDE, F32) for b in range(B)]
-        p_sb = [kept("p%d" % b, WIDE, BF16) for b in range(B)]
         z_sb = [kept("z%d" % b, WIDE, BF16) for b in range(B)]
         f_sb = [kept("f%d" % b, WIDE, BF16) for b in range(B)]
         o_sb = [kept("o%d" % b, WIDE, F32) for b in range(B)]
         dv_sb = kept("dv", WIDE, F32)
         v_sb = kept("v", WIDE, BF16)
         lse_sb = kept("lse", B * 8, F32)
-        neg_lse = kept("neg_lse", B * 8, F32)
+        lse_spread = kept("lse_spread", 2 * P, F32)
+        lse_rows = kept("lse_rows", 2 * P, F32)
+        neg_lse = kept("neg_lse", PACK, F32)
+        p_raw = kept("p_raw", WIDE, BF16)
+        ident_bf = kept("ident_bf", P, BF16)
         ident = kept("ident", P, F32)
         warm = kept("warm", 16, F32)
         codes = {}
@@ -62,22 +65,26 @@ def tile_quantumattentionblock_pb_v_kernel(tc, xwx, inp, V, x, u, lse, grad_out,
 
         half = WIDE // 2
 
-        def load(dst, src, parts=1):
-            step = WIDE // parts
-            for c in range(0, WIDE, step):
-                nc.sync.dma_start(out=dst[:, c : c + step], in_=rows4(src)[:, c : c + step])
+        def load(dst, src):
+            nc.sync.dma_start(out=dst[:], in_=rows4(src))
+
+        def load_part(dst, src, part, parts):
+            cols = slice(part * WIDE // parts, (part + 1) * WIDE // parts)
+            nc.sync.dma_start(out=dst[:, cols], in_=rows4(src)[:, cols])
 
         lse_view = lse_sb[:].rearrange("p (b e) -> p b e", e=8)[:, :, 0:PACK]
-        neg_view = neg_lse[:].rearrange("p (b e) -> p b e", e=8)[:, :, 0:PACK]
         nc.scalar.dma_start(out=lse_view, in_=lse.rearrange("b (p j) -> p b j", j=PACK))
-        load(g_sb[0], grad_out[0])
-        load(x_sb[0], xwx[0], 2)
-        load(g_sb[1], grad_out[1])
+        load_part(x_sb[0], xwx[0], 0, 4)
+        load_part(x_sb[0], xwx[0], 1, 4)
+        load_part(x_sb[0], xwx[0], 1, 2)
         load(x_sb[1], xwx[1])
+        load(g_sb[0], grad_out[0])
+        load_part(u_sb[0], u[0], 0, 2)
         load(x_sb[2], xwx[2])
-        load(g_sb[2], grad_out[2])
-        load(u_sb[0], u[0], 2)
+        load_part(u_sb[0], u[0], 1, 2)
+        load(g_sb[1], grad_out[1])
         load(v_sb, V)
+        load(g_sb[2], grad_out[2])
         load(i_sb[0], inp[0])
         load(u_sb[1], u[1])
         load(i_sb[1], inp[1])
@@ -87,17 +94,67 @@ def tile_quantumattentionblock_pb_v_kernel(tc, xwx, inp, V, x, u, lse, grad_out,
         nc.vector.memset(warm[:, 0:8], 0.0)
         nc.scalar.activation(out=warm[:, 8:16], in_=warm[:, 0:8], func=ACT.Exp)
         make_identity(nc, ident[:])
-        nc.vector.tensor_scalar(out=neg_view, in0=lse_view, scalar1=-1.0, scalar2=None, op0=ALU.mult)
+        make_identity(nc, ident_bf[:])
 
-        def probabilities(b):
+        def bank(tag):
+            return psum.tile([P, W], F32, name=tag)
+
+        def spread_lse():
+            turned = bank("b3")
+            nc.vector.tensor_scalar(out=neg_lse[:], in0=lse_sb[:, 0:PACK], scalar1=-1.0, scalar2=None, op0=ALU.mult)
+            for b in range(1, B):
+                cols = slice((b - 1) * P, b * P)
+                nc.vector.tensor_scalar(
+                    out=lse_spread[:, cols].rearrange("p (a j t) -> p a j t", j=PACK, t=PACK),
+                    in0=lse_sb[:, 8 * b : 8 * b + PACK].rearrange("p (a j t) -> p a j t", a=1, t=1).to_broadcast([P, 8, PACK, PACK]),
+                    scalar1=-1.0,
+                    scalar2=None,
+                    op0=ALU.mult,
+                )
+                nc.tensor.transpose(turned[:, cols], lse_spread[:, cols], ident[:])
+            nc.vector.tensor_copy(out=lse_rows[:], in_=turned[:, 0 : 2 * P])
+
+        def first_probabilities():
             for j in range(PACK):
                 cols = slice(j * W, (j + 1) * W)
                 nc.scalar.activation(
-                    out=p_sb[b][:, cols].rearrange("p (t m) -> p t m", t=PACK),
-                    in_=x_sb[b][:, cols].rearrange("p (m t) -> p t m", t=PACK),
+                    out=p_raw[:, cols].rearrange("p (t m) -> p t m", t=PACK),
+                    in_=x_sb[0][:, cols].rearrange("p (m t) -> p t m", t=PACK),
                     func=ACT.Exp,
-                    bias=neg_lse[:, 8 * b + j : 8 * b + j + 1],
+                    bias=neg_lse[:, j : j + 1],
                 )
+
+        def lse_into_bank(b, k):
+            acc = bank("%s%d" % ("b" if b == 2 else "a", k))
+            banks["sc", b, k] = acc
+            for q in range(4):
+                nc.tensor.matmul(
+                    out=acc[:, q * P : (q + 1) * P],
+                    lhsT=lse_rows[:, (b - 1) * P : b * P],
+                    rhs=ident[:],
+                    start=(q == 0),
+                    stop=False,
+                    is_transpose=True,
+                )
+
+        def scores_into_bank(b, k):
+            nc.tensor.matmul(
+                out=banks["sc", b, k][:],
+                lhsT=ident_bf[:],
+                rhs=x_sb[b][:].rearrange("p (j k a t) -> p k a j t", j=PACK, k=PACK, t=PACK)[:, k],
+                start=False,
+                stop=True,
+            )
+
+        def probabilities(b, k):
+            key = "p%d" % b
+            if k == 0:
+                grouped[key] = stage.tile([P, WIDE], BF16, name="grouped", align_bytes=64)
+            nc.scalar.activation(
+                out=grouped[key][:].rearrange("p (t k a j) -> p k t a j", t=PACK, k=PACK, j=PACK)[:, k],
+                in_=banks["sc", b, k][:].rearrange("p (a j t) -> p t a j", j=PACK, t=PACK),
+                func=ACT.Exp,
+            )
 
         def interleave(key, src, on_scalar=False):
             dst = stage.tile([P, WIDE], BF16, name="grouped", align_bytes=64)
@@ -109,6 +166,26 @@ def tile_quantumattentionblock_pb_v_kernel(tc, xwx, inp, V, x, u, lse, grad_out,
             else:
                 nc.vector.tensor_copy(out=out, in_=in_)
 
+        def interleave_inp(b):
+            dst = u_sb[b][:, half:WIDE].bitcast(BF16)
+            grouped["i%d" % b] = dst
+            nc.gpsimd.tensor_scalar(
+                out=dst.rearrange("p (c j) -> p c j", j=PACK),
+                in0=i_sb[b][:].rearrange("p (j c) -> p c j", j=PACK),
+                scalar1=1.0,
+                scalar2=0.0,
+                op0=ALU.mult,
+                op1=ALU.add,
+            )
+
+        def dz_stage(b):
+            interleave_inp(b)
+            for t in range(PACK):
+                dz(b, t)
+                if t % 2:
+                    transposes(b, t // 2)
+            feature_copy(b, 0)
+
         def quantize(key, fmt, part=0, parts=1):
             step = W // parts
             cols = slice(part * step, (part + 1) * step)
@@ -117,9 +194,6 @@ def tile_quantumattentionblock_pb_v_kernel(tc, xwx, inp, V, x, u, lse, grad_out,
                 scales=scales[key][:, cols],
                 in_=grouped[key][:, PACK * part * step : PACK * (part + 1) * step],
             )
-
-        def bank(tag):
-            return psum.tile([P, W], F32, name=tag)
 
         def product(acc, left, left_fmt, chunk, right, right_fmt, start=True, stop=True):
             cols = slice(chunk * P, (chunk + 1) * P)
@@ -135,7 +209,7 @@ def tile_quantumattentionblock_pb_v_kernel(tc, xwx, inp, V, x, u, lse, grad_out,
 
         def dh_products(b):
             for t in range(PACK):
-                banks["dh", t] = bank("wide%d" % t)
+                banks["dh", t] = bank("a%d" % t)
                 product(banks["dh", t], "p%d" % b, E4M3, t, "g%d" % b, E5M2)
 
         def square(b, h):
@@ -161,14 +235,15 @@ def tile_quantumattentionblock_pb_v_kernel(tc, xwx, inp, V, x, u, lse, grad_out,
 
         def transposes(b, pair):
             words = z_sb[b][:].bitcast(F32)
-            banks["tr", pair] = bank("turn%d" % pair)
+            banks["tr", pair] = bank("b%d" % (2 + pair))
             for q in range(4):
                 c = (4 * pair + q) * P
                 nc.tensor.transpose(banks["tr", pair][:, q * P : (q + 1) * P], words[:, c : c + P], ident[:])
 
         def feature_copy(b, pair):
             grouped["f%d" % b] = f_sb[b]
-            nc.scalar.copy(
+            copy = nc.scalar.copy if pair else nc.vector.tensor_copy
+            copy(
                 out=f_sb[b][:, pair * half : (pair + 1) * half].bitcast(F32).rearrange("p (t m h) -> p t m h", t=2, h=2),
                 in_=banks["tr", pair][:].rearrange("p (t h m) -> p t m h", t=2, h=2),
             )
@@ -191,7 +266,7 @@ def tile_quantumattentionblock_pb_v_kernel(tc, xwx, inp, V, x, u, lse, grad_out,
             )
 
         def dinp(b, t, on_vector=False):
-            acc = bank(("out0", "out1", "turn0", "turn1")[t])
+            acc = bank("b%d" % (t if b == B - 1 else t % 2))
             product(acc, "f%d" % b, E5M2, t, "v", E4M3)
             cols = slice(t * W, (t + 1) * W)
             if on_vector:
@@ -205,7 +280,7 @@ def tile_quantumattentionblock_pb_v_kernel(tc, xwx, inp, V, x, u, lse, grad_out,
 
         def dv_pass(c, b, last=False):
             if b == 0:
-                banks["dv", c] = bank("wide%d" % c)
+                banks["dv", c] = bank("a%d" % c)
             product(banks["dv", c], "t%d" % b, E5M2, c, "i%d" % b, E4M3, start=(b == 0), stop=last)
 
         def dv_out(c, on_vector):
@@ -216,97 +291,89 @@ def tile_quantumattentionblock_pb_v_kernel(tc, xwx, inp, V, x, u, lse, grad_out,
                 nc.scalar.copy(out=dv_sb[:, cols], in_=banks["dv", c][:])
             nc.sync.dma_start(out=rows4(out_1)[:, cols], in_=dv_sb[:, cols])
 
+        spread_lse()
+        first_probabilities()
+        interleave("p0", p_raw)
         interleave("g0", g_sb[0])
-        probabilities(0)
-        quantize("g0", E5M2)
-        interleave("g1", g_sb[1])
-        interleave("p0", p_sb[0])
-        quantize("g1", E5M2)
         quantize("p0", E4M3)
+        quantize("g0", E5M2)
+        for b in range(1, B):
+            for k in range(PACK):
+                lse_into_bank(b, k)
+                scores_into_bank(b, k)
+                probabilities(b, k)
+                if k == 2 - b:
+                    square(0, b - 1)
         dh_products(0)
-        probabilities(1)
-        interleave("p1", p_sb[1])
-        interleave("g2", g_sb[2])
-        quantize("p1", E4M3)
-        quantize("g2", E5M2)
-        probabilities(2)
-        square(0, 0)
-        square(0, 1)
         inverse_root(0, 0)
         inverse_root(0, 1)
-        interleave("p2", p_sb[2])
+        quantize("p1", E4M3)
+        interleave("g1", g_sb[1])
         interleave("v", v_sb)
+        quantize("g1", E5M2)
         quantize("p2", E4M3)
-        slope(0, 0)
+        interleave("g2", g_sb[2])
         quantize("v", E4M3)
+        slope(0, 0)
+        quantize("g2", E5M2)
         slope(0, 1)
         square(1, 0)
         square(1, 1)
         inverse_root(1, 0)
         inverse_root(1, 1)
-        for t in range(PACK):
-            dz(0, t)
-            if t % 2:
-                transposes(0, t // 2)
-        dh_products(1)
-        feature_copy(0, 0)
-        feature_copy(0, 1)
         square(2, 0)
+        dz_stage(0)
+        dh_products(1)
+        feature_copy(0, 1)
         square(2, 1)
-        slope(1, 0)
-        slope(1, 1)
-        quantize("f0", E5M2)
-        for t in range(PACK):
-            dinp(0, t)
-        store_dinp(0, 0, PACK)
-        for t in range(PACK):
-            dz(1, t)
-            if t % 2:
-                transposes(1, t // 2)
-        dh_products(2)
         inverse_root(2, 0)
-        feature_copy(1, 0)
-        feature_copy(1, 1)
         inverse_root(2, 1)
-        interleave("i0", i_sb[0], on_scalar=True)
-        token_interleave(0, 0)
-        token_interleave(0, 1)
-        token_quantize(0, 0)
-        token_quantize(0, 1)
+        slope(1, 0)
+        quantize("f0", E5M2)
+        slope(1, 1)
+        dinp(0, 0)
+        dinp(0, 1)
+        dz_stage(1)
+        feature_copy(1, 1)
+        dinp(0, 2)
+        dinp(0, 3)
+        store_dinp(0, 0, PACK)
+        dh_products(2)
+        token_interleave(0, 0, on_scalar=True)
         slope(2, 0)
+        quantize("i0", E4M3)
         quantize("f1", E5M2)
-        interleave("i1", i_sb[1])
         slope(2, 1)
-        quantize("i1", E4M3)
         for t in range(PACK):
             dinp(1, t)
         store_dinp(1, 0, PACK)
-        for t in range(PACK):
-            dz(2, t)
-            if t % 2:
-                transposes(2, t // 2)
-                feature_copy(2, t // 2)
-        token_interleave(2, 0, on_scalar=True)
-        token_interleave(2, 1, on_scalar=True)
-        quantize("i0", E4M3)
-        for c in range(PACK):
+        token_interleave(0, 1, on_scalar=True)
+        dz_stage(2)
+        feature_copy(2, 1)
+        token_quantize(0, 0)
+        quantize("f2", E5M2, 0, 2)
+        quantize("i1", E4M3)
+        quantize("f2", E5M2, 1, 2)
+        token_quantize(0, 1)
+        for c in range(2):
             dv_pass(c, 0)
-        interleave("i2", i_sb[2])
-        quantize("f2", E5M2)
-        quantize("i2", E4M3)
         for t in range(PACK):
             dinp(2, t)
             if t % 2:
                 store_dinp(2, t - 1, 2)
+        for c in range(2, 4):
+            dv_pass(c, 0)
         token_interleave(1, 0)
-        token_quantize(2, 0)
+        quantize("i2", E4M3)
         token_interleave(1, 1)
-        token_quantize(2, 1)
-        for c in range(PACK):
-            dv_pass(c, 2)
         token_quantize(1, 0)
+        token_interleave(2, 0)
         token_quantize(1, 1)
+        token_interleave(2, 1, on_scalar=True)
+        token_quantize(2, 0)
+        token_quantize(2, 1)
+        for b in (1, 2):
+            for c in range(PACK):
+                dv_pass(c, b, last=(b == 2))
         for c in range(PACK):
-            dv_pass(c, 1, last=True)
-        for c in range(PACK):
-            dv_out(c, on_vector=(c % 2 == 0))
+            dv_out(c, on_vector=(c % 2 == 1))

@@ -81,8 +81,8 @@ def tile_quantumattentionblock_pb_v_kernel(tc, xwx, inp, V, x, u, lse, grad_out,
         load(g_sb[0], grad_out[0])
         load_part(u_sb[0], u[0], 0, 2)
         load(x_sb[2], xwx[2])
-        load_part(u_sb[0], u[0], 1, 2)
         load(g_sb[1], grad_out[1])
+        load_part(u_sb[0], u[0], 1, 2)
         load(v_sb, V)
         load(g_sb[2], grad_out[2])
         load(i_sb[0], inp[0])
@@ -266,7 +266,7 @@ def tile_quantumattentionblock_pb_v_kernel(tc, xwx, inp, V, x, u, lse, grad_out,
             )
 
         def dinp(b, t, on_vector=False):
-            acc = bank("b%d" % (t if b == B - 1 else t % 2))
+            acc = bank("b%d" % ((0, 1, 0, 1), (0, 1, 3, 0), (0, 1, 2, 3))[b][t])
             product(acc, "f%d" % b, E5M2, t, "v", E4M3)
             cols = slice(t * W, (t + 1) * W)
             if on_vector:
@@ -302,29 +302,29 @@ def tile_quantumattentionblock_pb_v_kernel(tc, xwx, inp, V, x, u, lse, grad_out,
                 lse_into_bank(b, k)
                 scores_into_bank(b, k)
                 probabilities(b, k)
-                if k == 2 - b:
+                if k == 1:
                     square(0, b - 1)
         dh_products(0)
         inverse_root(0, 0)
         inverse_root(0, 1)
-        quantize("p1", E4M3)
         interleave("g1", g_sb[1])
-        interleave("v", v_sb)
+        quantize("p1", E4M3)
         quantize("g1", E5M2)
-        quantize("p2", E4M3)
+        interleave("v", v_sb)
         interleave("g2", g_sb[2])
         quantize("v", E4M3)
-        slope(0, 0)
+        quantize("p2", E4M3)
         quantize("g2", E5M2)
+        slope(0, 0)
         slope(0, 1)
         square(1, 0)
         square(1, 1)
         inverse_root(1, 0)
         inverse_root(1, 1)
-        square(2, 0)
         dz_stage(0)
         dh_products(1)
         feature_copy(0, 1)
+        square(2, 0)
         square(2, 1)
         inverse_root(2, 0)
         inverse_root(2, 1)
@@ -350,11 +350,12 @@ def tile_quantumattentionblock_pb_v_kernel(tc, xwx, inp, V, x, u, lse, grad_out,
         token_interleave(0, 1, on_scalar=True)
         dz_stage(2)
         feature_copy(2, 1)
+        token_interleave(1, 0, on_scalar=True)
         token_quantize(0, 0)
         quantize("f2", E5M2, 0, 2)
         quantize("i1", E4M3)
-        quantize("f2", E5M2, 1, 2)
         token_quantize(0, 1)
+        quantize("f2", E5M2, 1, 2)
         for c in range(2):
             dv_pass(c, 0)
         for t in range(PACK):
@@ -363,17 +364,16 @@ def tile_quantumattentionblock_pb_v_kernel(tc, xwx, inp, V, x, u, lse, grad_out,
                 store_dinp(2, t - 1, 2)
         for c in range(2, 4):
             dv_pass(c, 0)
-        token_interleave(1, 0)
-        quantize("i2", E4M3)
         token_interleave(1, 1)
+        quantize("i2", E4M3)
         token_quantize(1, 0)
         token_interleave(2, 0)
         token_quantize(1, 1)
-        token_interleave(2, 1, on_scalar=True)
         token_quantize(2, 0)
+        token_interleave(2, 1)
         token_quantize(2, 1)
         for b in (1, 2):
             for c in range(PACK):
                 dv_pass(c, b, last=(b == 2))
         for c in range(PACK):
-            dv_out(c, on_vector=(c % 2 == 1))
+            dv_out(c, on_vector=(c == 2))

from contextlib import ExitStack

import concourse.mybir as mybir
from concourse.masks import make_identity

B, N, D = 3, 512, 512
FLOPS = 3 * B * 2 * N * N * D
BYTES = 3 * B * N * D * 2 + D * D * 2 + B * N * D * 4 + B * N * 4 + B * N * D * 4 + D * D * 4

F32 = mybir.dt.float32
BF16 = mybir.dt.bfloat16
U32 = mybir.dt.uint32
U8 = mybir.dt.uint8
E4M3 = mybir.dt.float8_e4m3fn_x4
E5M2 = mybir.dt.float8_e5m2_x4
ACT = mybir.ActivationFunctionType
ALU = mybir.AluOpType

P = 128
PACK = 4
W = 512
WIDE = PACK * W
EPS = 1e-8


def tile_quantumattentionblock_pb_v_kernel(tc, xwx, inp, V, x, u, lse, grad_out, out_0, out_1):
    nc = tc.nc
    with ExitStack() as ctx:
        keep = ctx.enter_context(tc.tile_pool(name="keep", bufs=1))
        stage = ctx.enter_context(tc.tile_pool(name="stage", bufs=5))
        psum = ctx.enter_context(tc.psum_pool(name="psum", bufs=1))
        ctx.enter_context(tc.manual_schedule())

        def kept(name, width, dtype):
            return keep.tile([P, width], dtype, name=name, align_bytes=64)

        def rows4(ap):
            return ap.rearrange("(p j) w -> p (j w)", j=PACK)

        x_sb = [kept("x%d" % b, WIDE, BF16) for b in range(B)]
        g_sb = [kept("g%d" % b, WIDE, BF16) for b in range(B)]
        i_sb = [kept("i%d" % b, WIDE, BF16) for b in range(B)]
        u_sb = [kept("u%d" % b, WIDE, F32) for b in range(B)]
        s_sb = [kept("s%d" % b, WIDE, F32) for b in range(B)]
        z_sb = [kept("z%d" % b, WIDE, BF16) for b in range(B)]
        f_sb = [kept("f%d" % b, WIDE, BF16) for b in range(B)]
        o_sb = [kept("o%d" % b, WIDE, F32) for b in range(B)]
        dv_sb = kept("dv", WIDE, F32)
        v_sb = kept("v", WIDE, BF16)
        lse_sb = kept("lse", B * 8, F32)
        lse_spread = kept("lse_spread", 2 * P, F32)
        lse_rows = kept("lse_rows", 2 * P, F32)
        neg_lse = kept("neg_lse", PACK, F32)
        p_raw = kept("p_raw", WIDE, BF16)
        ident_bf = kept("ident_bf", P, BF16)
        ident = kept("ident", P, F32)
        warm = kept("warm", 16, F32)
        codes = {}
        scales = {}
        for key in ["v"] + [kind + str(b) for kind in "pgitf" for b in range(B)]:
            codes[key] = kept("codes_" + key, W, U32)
            scales[key] = kept("scales_" + key, W, U8)
        grouped = {}
        banks = {}

        half = WIDE // 2

        def load(dst, src):
            nc.sync.dma_start(out=dst[:], in_=rows4(src))

        def load_part(dst, src, part, parts):
            cols = slice(part * WIDE // parts, (part + 1) * WIDE // parts)
            nc.sync.dma_start(out=dst[:, cols], in_=rows4(src)[:, cols])

        lse_view = lse_sb[:].rearrange("p (b e) -> p b e", e=8)[:, :, 0:PACK]
        nc.scalar.dma_start(out=lse_view, in_=lse.rearrange("b (p j) -> p b j", j=PACK))
        load_part(x_sb[0], xwx[0], 0, 4)
        load_part(x_sb[0], xwx[0], 1, 4)
        load_part(x_sb[0], xwx[0], 1, 2)
        load(x_sb[1], xwx[1])
        load(g_sb[0], grad_out[0])
        load_part(u_sb[0], u[0], 0, 2)
        load(x_sb[2], xwx[2])
        load(g_sb[1], grad_out[1])
        load_part(u_sb[0], u[0], 1, 2)
        load(v_sb, V)
        load(g_sb[2], grad_out[2])
        load(i_sb[0], inp[0])
        load(u_sb[1], u[1])
        load(i_sb[1], inp[1])
        load(u_sb[2], u[2])
        load(i_sb[2], inp[2])

        nc.vector.memset(warm[:, 0:8], 0.0)
        nc.scalar.activation(out=warm[:, 8:16], in_=warm[:, 0:8], func=ACT.Exp)
        make_identity(nc, ident[:])
        make_identity(nc, ident_bf[:])

        def bank(tag):
            return psum.tile([P, W], F32, name=tag)

        def spread_lse():
            turned = bank("b3")
            nc.vector.tensor_scalar(out=neg_lse[:], in0=lse_sb[:, 0:PACK], scalar1=-1.0, scalar2=None, op0=ALU.mult)
            for b in range(1, B):
                cols = slice((b - 1) * P, b * P)
                nc.vector.tensor_scalar(
                    out=lse_spread[:, cols].rearrange("p (a j t) -> p a j t", j=PACK, t=PACK),
                    in0=lse_sb[:, 8 * b : 8 * b + PACK].rearrange("p (a j t) -> p a j t", a=1, t=1).to_broadcast([P, 8, PACK, PACK]),
                    scalar1=-1.0,
                    scalar2=None,
                    op0=ALU.mult,
                )
                nc.tensor.transpose(turned[:, cols], lse_spread[:, cols], ident[:])
            nc.vector.tensor_copy(out=lse_rows[:], in_=turned[:, 0 : 2 * P])

        def first_probabilities():
            for j in range(PACK):
                cols = slice(j * W, (j + 1) * W)
                nc.scalar.activation(
                    out=p_raw[:, cols].rearrange("p (t m) -> p t m", t=PACK),
                    in_=x_sb[0][:, cols].rearrange("p (m t) -> p t m", t=PACK),
                    func=ACT.Exp,
                    bias=neg_lse[:, j : j + 1],
                )

        def lse_into_bank(b, k):
            acc = bank("%s%d" % ("b" if b == 2 else "a", k))
            banks["sc", b, k] = acc
            for q in range(4):
                nc.tensor.matmul(
                    out=acc[:, q * P : (q + 1) * P],
                    lhsT=lse_rows[:, (b - 1) * P : b * P],
                    rhs=ident[:],
                    start=(q == 0),
                    stop=False,
                    is_transpose=True,
                )

        def scores_into_bank(b, k):
            nc.tensor.matmul(
                out=banks["sc", b, k][:],
                lhsT=ident_bf[:],
                rhs=x_sb[b][:].rearrange("p (j k a t) -> p k a j t", j=PACK, k=PACK, t=PACK)[:, k],
                start=False,
                stop=True,
            )

        def probabilities(b, k):
            key = "p%d" % b
            if k == 0:
                grouped[key] = stage.tile([P, WIDE], BF16, name="grouped", align_bytes=64)
            nc.scalar.activation(
                out=grouped[key][:].rearrange("p (t k a j) -> p k t a j", t=PACK, k=PACK, j=PACK)[:, k],
                in_=banks["sc", b, k][:].rearrange("p (a j t) -> p t a j", j=PACK, t=PACK),
                func=ACT.Exp,
            )

        def interleave(key, src, on_scalar=False):
            dst = stage.tile([P, WIDE], BF16, name="grouped", align_bytes=64)
            grouped[key] = dst
            out = dst[:].rearrange("p (c i j) -> p c j i", i=4, j=PACK)
            in_ = src[:].rearrange("p (j c i) -> p c j i", i=4, j=PACK)
            if on_scalar:
                nc.scalar.copy(out=out, in_=in_)
            else:
                nc.vector.tensor_copy(out=out, in_=in_)

        def interleave_inp(b):
            dst = u_sb[b][:, half:WIDE].bitcast(BF16)
            grouped["i%d" % b] = dst
            nc.gpsimd.tensor_scalar(
                out=dst.rearrange("p (c j) -> p c j", j=PACK),
                in0=i_sb[b][:].rearrange("p (j c) -> p c j", j=PACK),
                scalar1=1.0,
                scalar2=0.0,
                op0=ALU.mult,
                op1=ALU.add,
            )

        def dz_stage(b):
            interleave_inp(b)
            for t in range(PACK):
                dz(b, t)
                if t % 2:
                    transposes(b, t // 2)
            feature_copy(b, 0)

        def quantize(key, fmt, part=0, parts=1):
            step = W // parts
            cols = slice(part * step, (part + 1) * step)
            nc.vector.quantize_mx(
                out=codes[key][:, cols].bitcast(fmt),
                scales=scales[key][:, cols],
                in_=grouped[key][:, PACK * part * step : PACK * (part + 1) * step],
            )

        def product(acc, left, left_fmt, chunk, right, right_fmt, start=True, stop=True):
            cols = slice(chunk * P, (chunk + 1) * P)
            nc.tensor.matmul_mx(
                out=acc[:],
                lhsT=codes[left][:, cols].bitcast(left_fmt),
                lhsT_scale=scales[left][:, cols],
                rhs=codes[right][:].bitcast(right_fmt),
                rhs_scale=scales[right][:],
                start=start,
                stop=stop,
            )

        def dh_products(b):
            for t in range(PACK):
                banks["dh", t] = bank("a%d" % t)
                product(banks["dh", t], "p%d" % b, E4M3, t, "g%d" % b, E5M2)

        def square(b, h):
            cols = slice(h * half, (h + 1) * half)
            nc.scalar.activation(out=s_sb[b][:, cols], in_=u_sb[b][:, cols], func=ACT.Square)

        def inverse_root(b, h):
            cols = slice(h * half, (h + 1) * half)
            nc.scalar.activation(out=s_sb[b][:, cols], in_=s_sb[b][:, cols], func=ACT.Abs_reciprocal_sqrt, bias=EPS)

        def slope(b, h):
            cols = slice(h * half, (h + 1) * half)
            nc.vector.tensor_tensor(out=s_sb[b][:, cols], in0=u_sb[b][:, cols], in1=s_sb[b][:, cols], op=ALU.mult)

        def dz(b, t):
            cols = slice(t * W, (t + 1) * W)
            nc.vector.tensor_tensor(
                out=z_sb[b][:, cols].rearrange("p (h w e) -> p h w e", h=2, e=2),
                in0=banks["dh", t][:].rearrange("p (w h e) -> p h w e", h=2, e=2),
                in1=s_sb[b][:, cols].rearrange("p (w h e) -> p h w e", h=2, e=2),
                op=ALU.mult,
            )

        def transposes(b, pair):
            words = z_sb[b][:].bitcast(F32)
            banks["tr", pair] = bank("b%d" % (2 + pair))
            for q in range(4):
                c = (4 * pair + q) * P
                nc.tensor.transpose(banks["tr", pair][:, q * P : (q + 1) * P], words[:, c : c + P], ident[:])

        def feature_copy(b, pair):
            grouped["f%d" % b] = f_sb[b]
            copy = nc.scalar.copy if pair else nc.vector.tensor_copy
            copy(
                out=f_sb[b][:, pair * half : (pair + 1) * half].bitcast(F32).rearrange("p (t m h) -> p t m h", t=2, h=2),
                in_=banks["tr", pair][:].rearrange("p (t h m) -> p t m h", t=2, h=2),
            )

        def token_interleave(b, h, on_scalar=False):
            key = "t%d%d" % (b, h)
            grouped[key] = stage.tile([P, half], BF16, name="grouped_half", align_bytes=64)
            copy = nc.scalar.copy if on_scalar else nc.vector.tensor_copy
            copy(
                out=grouped[key][:].rearrange("p (e c a t) -> p c t a e", e=2, a=2, t=PACK),
                in_=z_sb[b][:].rearrange("p (t h c a e) -> p h c t a e", t=PACK, h=2, a=2, e=2)[:, h],
            )

        def token_quantize(b, h):
            cols = slice(h * W // 2, (h + 1) * W // 2)
            nc.vector.quantize_mx(
                out=codes["t%d" % b][:, cols].bitcast(E5M2),
                scales=scales["t%d" % b][:, cols],
                in_=grouped["t%d%d" % (b, h)][:],
            )

        def dinp(b, t, on_vector=False):
            acc = bank("b%d" % ((0, 1, 0, 1), (0, 1, 3, 0), (0, 1, 2, 3))[b][t])
            product(acc, "f%d" % b, E5M2, t, "v", E4M3)
            cols = slice(t * W, (t + 1) * W)
            if on_vector:
                nc.vector.tensor_copy(out=o_sb[b][:, cols], in_=acc[:])
            else:
                nc.scalar.copy(out=o_sb[b][:, cols], in_=acc[:])

        def store_dinp(b, first, count):
            cols = slice(first * W, (first + count) * W)
            nc.sync.dma_start(out=rows4(out_0[b])[:, cols], in_=o_sb[b][:, cols])

        def dv_pass(c, b, last=False):
            if b == 0:
                banks["dv", c] = bank("a%d" % c)
            product(banks["dv", c], "t%d" % b, E5M2, c, "i%d" % b, E4M3, start=(b == 0), stop=last)

        def dv_out(c, on_vector):
            cols = slice(c * W, (c + 1) * W)
            if on_vector:
                nc.vector.tensor_copy(out=dv_sb[:, cols], in_=banks["dv", c][:])
            else:
                nc.scalar.copy(out=dv_sb[:, cols], in_=banks["dv", c][:])
            nc.sync.dma_start(out=rows4(out_1)[:, cols], in_=dv_sb[:, cols])

        spread_lse()
        first_probabilities()
        interleave("p0", p_raw)
        interleave("g0", g_sb[0])
        quantize("p0", E4M3)
        quantize("g0", E5M2)
        for b in range(1, B):
            for k in range(PACK):
                lse_into_bank(b, k)
                scores_into_bank(b, k)
                probabilities(b, k)
                if k == 1:
                    square(0, b - 1)
        dh_products(0)
        inverse_root(0, 0)
        inverse_root(0, 1)
        interleave("g1", g_sb[1])
        quantize("p1", E4M3)
        quantize("g1", E5M2)
        interleave("v", v_sb)
        interleave("g2", g_sb[2])
        quantize("v", E4M3)
        quantize("p2", E4M3)
        quantize("g2", E5M2)
        slope(0, 0)
        slope(0, 1)
        square(1, 0)
        square(1, 1)
        inverse_root(1, 0)
        inverse_root(1, 1)
        dz_stage(0)
        dh_products(1)
        feature_copy(0, 1)
        square(2, 0)
        square(2, 1)
        inverse_root(2, 0)
        inverse_root(2, 1)
        slope(1, 0)
        quantize("f0", E5M2)
        slope(1, 1)
        dinp(0, 0)
        dinp(0, 1)
        dz_stage(1)
        feature_copy(1, 1)
        dinp(0, 2)
        dinp(0, 3)
        store_dinp(0, 0, PACK)
        dh_products(2)
        token_interleave(0, 0, on_scalar=True)
        slope(2, 0)
        quantize("i0", E4M3)
        quantize("f1", E5M2)
        slope(2, 1)
        for t in range(PACK):
            dinp(1, t)
        store_dinp(1, 0, PACK)
        token_interleave(0, 1, on_scalar=True)
        dz_stage(2)
        feature_copy(2, 1)
        token_interleave(1, 0, on_scalar=True)
        token_quantize(0, 0)
        quantize("f2", E5M2, 0, 2)
        quantize("i1", E4M3)
        token_quantize(0, 1)
        quantize("f2", E5M2, 1, 2)
        for c in range(2):
            dv_pass(c, 0)
        for t in range(PACK):
            dinp(2, t)
            if t % 2:
                store_dinp(2, t - 1, 2)
        for c in range(2, 4):
            dv_pass(c, 0)
        token_interleave(1, 1)
        quantize("i2", E4M3)
        token_quantize(1, 0)
        token_interleave(2, 0)
        token_quantize(1, 1)
        token_quantize(2, 0)
        token_interleave(2, 1)
        token_quantize(2, 1)
        for b in (1, 2):
            for c in range(PACK):
                dv_pass(c, b, last=(b == 2))
        for c in range(PACK):
            dv_out(c, on_vector=(c == 2))
